import numpy as np
import ml_dtypes


def mxq(x, axis, fmt="e4m3"):
    dtype, down = {"e4m3": (ml_dtypes.float8_e4m3fn, 7), "e5m2": (ml_dtypes.float8_e5m2, 14)}[fmt]
    v = np.moveaxis(np.asarray(x, np.float32).astype(ml_dtypes.bfloat16).astype(np.float64), axis, -1)
    blocks = v.reshape(v.shape[:-1] + (-1, 32))
    amax = np.abs(blocks).max(-1, keepdims=True)
    byte = np.maximum(np.where(amax > 0, np.frexp(amax)[1] - 1 + 127, 0) - down, 1)
    scale = np.exp2(byte - 127.0)
    codes = (blocks / scale).astype(np.float32).astype(dtype).astype(np.float64)
    return np.moveaxis((codes * scale).reshape(v.shape), -1, axis)


WIDE = False


def mx_kscale(k):
    if not WIDE:
        return np.ones(k)
    levels = np.array([10, -10, 5, -5, 0])
    a = np.random.permutation(np.resize(levels, k // 512 * 4)).reshape(k // 512, 4)
    idx = np.arange(k)
    return np.exp2(a[idx // 512, idx % 128 // 32])


BF16 = ml_dtypes.bfloat16


def bf(x):
    return np.asarray(x, np.float32).astype(BF16)


def f64(x):
    return np.asarray(x).astype(np.float64)


B, IN, H, NS, SS, CS, NA = 6144, 256, 1024, 4, 4, 32, 3
NC = NS * CS


def setup_inputs():
    s = mx_kscale(H)
    return {
        "h": bf(np.tanh(np.random.standard_normal((B, H))) * s),
        "act_logits": bf(np.random.standard_normal((B, NS * NA)) * 1.5),
        "stacks": bf(np.random.standard_normal((B, NS, SS, CS)) * 1.5),
        "W_push": bf(np.random.standard_normal((NC, H)) * 5.0 / np.sqrt(H) / s),
        "b_push": bf(np.random.standard_normal(NC) * 0.7),
    }


def reference(h, act_logits, stacks, W_push, b_push):
    st = f64(stacks)
    push = ((mxq(f64(h), 1, "e4m3") @ mxq(f64(W_push), 1, "e4m3").T) + f64(b_push)).reshape(B, NS, CS)
    lg = f64(act_logits)
    e = np.exp(lg - lg.max(-1, keepdims=True))
    act = (e / e.sum(-1, keepdims=True)).reshape(B, NS, NA)
    pa, po, no = act[..., 0][..., None], act[..., 1][..., None], act[..., 2][..., None]
    top_new = pa * push + po * st[:, :, 1, :] + no * st[:, :, 0, :]
    zeros_tail = np.zeros((B, NS, 1, CS))
    pop_rest = np.concatenate([st[:, :, 2:, :], zeros_tail], axis=2)
    rest = (pa[:, :, :, None] * st[:, :, :-1, :]
            + po[:, :, :, None] * pop_rest
            + no[:, :, :, None] * st[:, :, 1:, :])
    return np.concatenate([top_new[:, :, None, :], rest], axis=2)

@@ -1,0 +1,235 @@
+from contextlib import ExitStack
+
+import concourse.mybir as mybir
+from concourse.masks import make_identity
+
+F32 = mybir.dt.float32
+BF16 = mybir.dt.bfloat16
+U32 = mybir.dt.uint32
+U8 = mybir.dt.uint8
+FP8X4 = mybir.dt.float8_e4m3fn_x4
+ALU = mybir.AluOpType
+ACT = mybir.ActivationFunctionType
+AX = mybir.AxisListType
+
+P = 128
+B, H, NS, SS, CS, NA = 6144, 1024, 4, 4, 32, 3
+NC = NS * CS
+ROW = NS * SS * CS
+TILES = B // P
+NL = NS * NA
+FLOPS = 2 * B * H * NC
+
+SIZES = [1, 1, 2] + [4] * 10 + [2, 1, 1]
+HEAD_TILES = 4
+SCALAR_TOP = (4, 6, 8, 10, 12)
+
+
+def tile_stackrnncore_pa_t_kernel(tc, h, act_logits, stacks, W_push, b_push, out):
+    nc = tc.nc
+    h_v = h.rearrange("(p t) k -> p (t k)", t=TILES)
+    st_v = stacks.rearrange("(p t) n i c -> p (t n i c)", t=TILES)
+    out_v = out.rearrange("(p t) n i c -> p (t n i c)", t=TILES)
+    lg_v = act_logits.rearrange("(p t) j -> p (t j)", t=TILES)
+    starts = [sum(SIZES[:g]) for g in range(len(SIZES))]
+    n_groups = len(SIZES)
+
+    with ExitStack() as ctx:
+        const = ctx.enter_context(tc.tile_pool(name="const", bufs=1))
+        hpool = ctx.enter_context(tc.tile_pool(name="hpool", bufs=5))
+        spool = ctx.enter_context(tc.tile_pool(name="spool", bufs=7))
+        gpool = ctx.enter_context(tc.tile_pool(name="gpool", bufs=3))
+        cpool = ctx.enter_context(tc.tile_pool(name="cpool", bufs=2))
+        upool = ctx.enter_context(tc.tile_pool(name="upool", bufs=2))
+        opool = ctx.enter_context(tc.tile_pool(name="opool", bufs=5))
+        xt_ps = ctx.enter_context(tc.psum_pool(name="xt_ps", bufs=4))
+        acc_ps = ctx.enter_context(tc.psum_pool(name="acc_ps", bufs=2))
+        u_ps = ctx.enter_context(tc.psum_pool(name="u_ps", bufs=2))
+
+        lg = const.tile([P, TILES * NL], BF16)
+        nc.sync.dma_start(out=lg[:], in_=lg_v)
+        w_sb = const.tile([P, H], BF16)
+        nc.sync.dma_start(out=w_sb[:], in_=W_push)
+        b_sb = const.tile([P, 1], BF16)
+        nc.sync.dma_start(out=b_sb[:], in_=b_push.rearrange("(p o) -> p o", o=1))
+
+        ident = const.tile([P, P], F32)
+        make_identity(nc, ident[:])
+
+        x_tiles = {}
+        s_tiles = {}
+        g_tiles = {}
+        u_tiles = {}
+        o_tiles = {}
+
+        def load(g):
+            t0, gt = starts[g], SIZES[g]
+            x_sb = hpool.tile([P, gt * H], BF16, tag="x", name="x_sb")
+            nc.sync.dma_start(out=x_sb[:], in_=h_v[:, t0 * H:(t0 + gt) * H])
+            s_sb = spool.tile([P, gt * ROW], BF16, tag="s", name="s_sb")
+            nc.sync.dma_start(out=s_sb[:], in_=st_v[:, t0 * ROW:(t0 + gt) * ROW])
+            x_tiles[g] = x_sb
+            s_tiles[g] = s_sb
+
+        load(0)
+        load(1)
+
+        ww = w_sb[:].bitcast(F32)
+        wt = xt_ps.tile([P, 2, 2, P], F32, tag="xt", name="wt")
+        for gg in range(2):
+            for u in range(2):
+                c0 = 256 * gg + 128 * u
+                nc.tensor.transpose(wt[:, gg, u, :], ww[:, c0:c0 + P], ident[:])
+        wgrouped = const.tile([P, 2 * P * 4], BF16, align_bytes=64)
+        nc.scalar.copy(
+            out=wgrouped[:].bitcast(F32).rearrange("p (g r u) -> p g r u", g=2, u=2),
+            in_=wt[:].rearrange("p g u r -> p g r u"),
+        )
+        wcodes = const.tile([P, 2 * P], U32, align_bytes=64)
+        wscl = const.tile([P, 2 * P], U8, align_bytes=64)
+        nc.vector.quantize_mx(out=wcodes[:].bitcast(FP8X4), scales=wscl[:], in_=wgrouped[:])
+        bias32 = const.tile([P, 1], F32)
+        nc.vector.tensor_copy(out=bias32[:], in_=b_sb[:])
+
+        mx = const.tile([P, TILES], F32)
+        dif = const.tile([P, TILES * NL], F32)
+        ex = const.tile([P, TILES * NL], F32)
+        sm = const.tile([P, TILES], F32)
+        rs = const.tile([P, TILES], F32)
+        act = const.tile([P, TILES * NL], F32)
+
+        def softmax(ta, tb):
+            n_t = tb - ta
+            cols = slice(ta * NL, tb * NL)
+            lg3 = lg[:, cols].rearrange("p (t j) -> p t j", j=NL)
+            dif3 = dif[:, cols].rearrange("p (t j) -> p t j", j=NL)
+            ex3 = ex[:, cols].rearrange("p (t j) -> p t j", j=NL)
+            act3 = act[:, cols].rearrange("p (t j) -> p t j", j=NL)
+            nc.vector.tensor_reduce(out=mx[:, ta:tb], in_=lg3, axis=AX.X, op=ALU.max)
+            nc.vector.tensor_tensor(
+                out=dif3, in0=lg3, in1=mx[:, ta:tb].unsqueeze(2).to_broadcast([P, n_t, NL]), op=ALU.subtract
+            )
+            nc.scalar.activation(out=ex[:, cols], in_=dif[:, cols], func=ACT.Exp)
+            nc.vector.tensor_reduce(out=sm[:, ta:tb], in_=ex3, axis=AX.X, op=ALU.add)
+            nc.vector.reciprocal(out=rs[:, ta:tb], in_=sm[:, ta:tb])
+            nc.vector.tensor_tensor(
+                out=act3, in0=ex3, in1=rs[:, ta:tb].unsqueeze(2).to_broadcast([P, n_t, NL]), op=ALU.mult
+            )
+
+        def stage1(g):
+            gt = SIZES[g]
+            xw = x_tiles[g][:].bitcast(F32)
+            grouped = gpool.tile([P, 2 * gt * P * 4], BF16, align_bytes=64, tag="grp", name="grouped")
+            gw = grouped[:].bitcast(F32).rearrange("p (g j r u) -> p g j r u", g=2, j=gt, u=2)
+            for j in range(gt):
+                xt = xt_ps.tile([P, 2, 2, P], F32, tag="xt", name="xt")
+                for gg in range(2):
+                    for u in range(2):
+                        c0 = j * (H // 2) + 256 * gg + 128 * u
+                        nc.tensor.transpose(xt[:, gg, u, :], xw[:, c0:c0 + P], ident[:])
+                nc.scalar.copy(out=gw[:, :, j, :, :], in_=xt[:].rearrange("p g u r -> p g r u"))
+            g_tiles[g] = grouped
+
+        def stage2(g):
+            t0, gt = starts[g], SIZES[g]
+            n_cols = gt * P
+            grouped = g_tiles[g]
+            codes = cpool.tile([P, 2 * n_cols], U32, align_bytes=64, tag="codes", name="codes")
+            scl = cpool.tile([P, 2 * n_cols], U8, align_bytes=64, tag="scl", name="scl")
+            nc.vector.quantize_mx(out=codes[:].bitcast(FP8X4), scales=scl[:], in_=grouped[:])
+            acc = acc_ps.tile([P, n_cols], F32, tag="acc", name="acc")
+            for gg in range(2):
+                nc.tensor.matmul_mx(
+                    out=acc[:],
+                    lhsT=wcodes[:, gg * P:(gg + 1) * P].bitcast(FP8X4),
+                    lhsT_scale=wscl[:, gg * P:(gg + 1) * P],
+                    rhs=codes[:, gg * n_cols:(gg + 1) * n_cols].bitcast(FP8X4),
+                    rhs_scale=scl[:, gg * n_cols:(gg + 1) * n_cols],
+                    start=(gg == 0),
+                    stop=(gg == 1),
+                )
+            ut = upool.tile([P, n_cols], F32, tag="ut", name="ut")
+            nc.scalar.activation(out=ut[:], in_=acc[:], func=ACT.Identity, bias=bias32[:, 0:1], scale=1.0)
+            up = u_ps.tile([P, n_cols], F32, tag="up", name="up")
+            for j in range(gt):
+                nc.tensor.transpose(up[:, j * P:(j + 1) * P], ut[:, j * P:(j + 1) * P], ident[:])
+            u_tiles[g] = up
+            s_sb = s_tiles[g]
+            o_sb = opool.tile([P, gt * ROW], F32, tag="o", name="o_sb")
+            o_tiles[g] = o_sb
+            for q in range(gt * NS):
+                base = q * P
+                k = t0 * NL + q * NA
+                nc.scalar.activation(
+                    out=o_sb[:, base + CS:base + P],
+                    in_=s_sb[:, base:base + P - CS],
+                    func=ACT.Copy,
+                    scale=act[:, k:k + 1],
+                )
+
+        def stage3(g):
+            t0, gt = starts[g], SIZES[g]
+            s_sb, o_sb, up = s_tiles[g], o_tiles[g], u_tiles[g]
+            if g in SCALAR_TOP:
+                for q in range(gt * NS):
+                    k = t0 * NL + q * NA
+                    nc.scalar.activation(
+                        out=o_sb[:, q * P:q * P + CS],
+                        in_=up[:, q * CS:(q + 1) * CS],
+                        func=ACT.Copy,
+                        scale=act[:, k:k + 1],
+                    )
+            else:
+                pa_bc = (
+                    act[:, t0 * NL:(t0 + gt) * NL]
+                    .rearrange("p (q a) -> p q a", a=NA)[:, :, 0:1]
+                    .to_broadcast([P, gt * NS, CS])
+                )
+                nc.vector.tensor_tensor(
+                    out=o_sb[:].rearrange("p (q i c) -> p q i c", i=SS, c=CS)[:, :, 0, :],
+                    in0=up[:].rearrange("p (q c) -> p q c", c=CS),
+                    in1=pa_bc,
+                    op=ALU.mult,
+                )
+            for j in range(gt):
+                for n in range(NS):
+                    q = j * NS + n
+                    base = q * P
+                    k = t0 * NL + q * NA + 2
+                    nc.vector.scalar_tensor_tensor(
+                        out=o_sb[:, base:base + P],
+                        in0=s_sb[:, base:base + P],
+                        scalar=act[:, k:k + 1],
+                        in1=o_sb[:, base:base + P],
+                        op0=ALU.mult,
+                        op1=ALU.add,
+                    )
+                for n in range(NS):
+                    q = j * NS + n
+                    base = q * P
+                    k = t0 * NL + q * NA + 1
+                    nc.vector.scalar_tensor_tensor(
+                        out=o_sb[:, base:base + P - CS],
+                        in0=s_sb[:, base + CS:base + P],
+                        scalar=act[:, k:k + 1],
+                        in1=o_sb[:, base:base + P - CS],
+                        op0=ALU.mult,
+                        op1=ALU.add,
+                    )
+            nc.sync.dma_start(out=out_v[:, t0 * ROW:(t0 + gt) * ROW], in_=o_sb[:])
+
+        softmax(0, HEAD_TILES)
+        stage1(0)
+        load(2)
+        stage2(0)
+        stage1(1)
+        load(3)
+        softmax(HEAD_TILES, TILES)
+        for g in range(n_groups):
+            if g + 4 < n_groups:
+                load(g + 4)
+            if g + 1 < n_groups:
+                stage2(g + 1)
+            if g + 2 < n_groups:
+                stage1(g + 2)
+            stage3(g)

@@ -20,9 +20,12 @@ TILES = B // P
 NL = NS * NA
 FLOPS = 2 * B * H * NC
 
-SIZES = [1, 1, 2] + [4] * 10 + [2, 1, 1]
+SIZES = [1, 1, 1, 1] + [2] * 21 + [1, 1]
+CHUNKS = [1, 1, 2] + [4] * 11
 HEAD_TILES = 4
-SCALAR_TOP = (4, 6, 8, 10, 12)
+X_BUFS = 6
+S_BUFS = 8
+O_BUFS = 5
 
 
 def tile_stackrnncore_pa_t_kernel(tc, h, act_logits, stacks, W_push, b_push, out):
@@ -31,20 +34,39 @@ def tile_stackrnncore_pa_t_kernel(tc, h, act_logits, stacks, W_push, b_push, out
     st_v = stacks.rearrange("(p t) n i c -> p (t n i c)", t=TILES)
     out_v = out.rearrange("(p t) n i c -> p (t n i c)", t=TILES)
     lg_v = act_logits.rearrange("(p t) j -> p (t j)", t=TILES)
-    starts = [sum(SIZES[:g]) for g in range(len(SIZES))]
     n_groups = len(SIZES)
+    n_chunks = len(CHUNKS)
+    g_start = [sum(SIZES[:g]) for g in range(n_groups)]
+    c_start = [sum(CHUNKS[:c]) for c in range(n_chunks)]
+    g_chunk = [max(c for c in range(n_chunks) if c_start[c] <= g_start[g]) for g in range(n_groups)]
+    c_last = [max(g for g in range(n_groups) if g_chunk[g] == c) for c in range(n_chunks)]
+    c_first = [min(g for g in range(n_groups) if g_chunk[g] == c) for c in range(n_chunks)]
+
+    def scalar_top(g):
+        return g % 3 != 0
 
     with ExitStack() as ctx:
         const = ctx.enter_context(tc.tile_pool(name="const", bufs=1))
-        hpool = ctx.enter_context(tc.tile_pool(name="hpool", bufs=5))
-        spool = ctx.enter_context(tc.tile_pool(name="spool", bufs=7))
-        gpool = ctx.enter_context(tc.tile_pool(name="gpool", bufs=3))
+        hpool = ctx.enter_context(tc.tile_pool(name="hpool", bufs=X_BUFS))
+        spool = ctx.enter_context(tc.tile_pool(name="spool", bufs=S_BUFS))
+        gpool = ctx.enter_context(tc.tile_pool(name="gpool", bufs=2))
         cpool = ctx.enter_context(tc.tile_pool(name="cpool", bufs=2))
         upool = ctx.enter_context(tc.tile_pool(name="upool", bufs=2))
-        opool = ctx.enter_context(tc.tile_pool(name="opool", bufs=5))
+        opool = ctx.enter_context(tc.tile_pool(name="opool", bufs=O_BUFS))
         xt_ps = ctx.enter_context(tc.psum_pool(name="xt_ps", bufs=4))
         acc_ps = ctx.enter_context(tc.psum_pool(name="acc_ps", bufs=2))
         u_ps = ctx.enter_context(tc.psum_pool(name="u_ps", bufs=2))
+        ctx.enter_context(tc.manual_schedule())
+
+        x_tiles = {}
+        s_tiles = {}
+        o_tiles = {}
+        xt_tiles = {}
+        grp_tiles = {}
+        code_tiles = {}
+        acc_tiles = {}
+        ut_tiles = {}
+        up_tiles = {}
 
         lg = const.tile([P, TILES * NL], BF16)
         nc.sync.dma_start(out=lg[:], in_=lg_v)
@@ -53,26 +75,193 @@ def tile_stackrnncore_pa_t_kernel(tc, h, act_logits, stacks, W_push, b_push, out
         b_sb = const.tile([P, 1], BF16)
         nc.sync.dma_start(out=b_sb[:], in_=b_push.rearrange("(p o) -> p o", o=1))
 
+        def load(c):
+            t0, ct = c_start[c], CHUNKS[c]
+            x_sb = hpool.tile([P, ct * H], BF16, tag="x", name="x_sb")
+            nc.sync.dma_start(out=x_sb[:], in_=h_v[:, t0 * H:(t0 + ct) * H])
+            s_sb = spool.tile([P, ct * ROW], BF16, tag="s", name="s_sb")
+            nc.sync.dma_start(out=s_sb[:], in_=st_v[:, t0 * ROW:(t0 + ct) * ROW])
+            x_tiles[c] = x_sb
+            s_tiles[c] = s_sb
+
+        for c in range(X_BUFS):
+            load(c)
+
         ident = const.tile([P, P], F32)
         make_identity(nc, ident[:])
 
-        x_tiles = {}
-        s_tiles = {}
-        g_tiles = {}
-        u_tiles = {}
-        o_tiles = {}
+        mx = const.tile([P, TILES], F32)
+        dif = const.tile([P, TILES * NL], F32)
+        ex = const.tile([P, TILES * NL], F32)
+        sm = const.tile([P, TILES], F32)
+        rs = const.tile([P, TILES], F32)
+        act = const.tile([P, TILES * NL], F32)
 
-        def load(g):
-            t0, gt = starts[g], SIZES[g]
-            x_sb = hpool.tile([P, gt * H], BF16, tag="x", name="x_sb")
-            nc.sync.dma_start(out=x_sb[:], in_=h_v[:, t0 * H:(t0 + gt) * H])
-            s_sb = spool.tile([P, gt * ROW], BF16, tag="s", name="s_sb")
-            nc.sync.dma_start(out=s_sb[:], in_=st_v[:, t0 * ROW:(t0 + gt) * ROW])
-            x_tiles[g] = x_sb
-            s_tiles[g] = s_sb
+        def by_row(t, ta, tb):
+            return t[:, ta * NL:tb * NL].rearrange("p (t j) -> p t j", j=NL)
 
-        load(0)
-        load(1)
+        def softmax_shift(ta, tb):
+            nc.vector.tensor_reduce(out=mx[:, ta:tb], in_=by_row(lg, ta, tb), axis=AX.X, op=ALU.max)
+            nc.vector.tensor_tensor(
+                out=by_row(dif, ta, tb),
+                in0=by_row(lg, ta, tb),
+                in1=mx[:, ta:tb].unsqueeze(2).to_broadcast([P, tb - ta, NL]),
+                op=ALU.subtract,
+            )
+
+        def softmax_exp(ta, tb):
+            nc.scalar.activation(out=ex[:, ta * NL:tb * NL], in_=dif[:, ta * NL:tb * NL], func=ACT.Exp)
+
+        def softmax_norm(ta, tb):
+            nc.vector.tensor_reduce(out=sm[:, ta:tb], in_=by_row(ex, ta, tb), axis=AX.X, op=ALU.add)
+            nc.vector.reciprocal(out=rs[:, ta:tb], in_=sm[:, ta:tb])
+            nc.vector.tensor_tensor(
+                out=by_row(act, ta, tb),
+                in0=by_row(ex, ta, tb),
+                in1=rs[:, ta:tb].unsqueeze(2).to_broadcast([P, tb - ta, NL]),
+                op=ALU.mult,
+            )
+
+        def transposes(g):
+            c, gt = g_chunk[g], SIZES[g]
+            xw = x_tiles[c][:].bitcast(F32)
+            for j in range(gt):
+                xt = xt_ps.tile([P, 2, 2, P], F32, tag="xt", name="xt")
+                for gg in range(2):
+                    for u in range(2):
+                        c0 = (g_start[g] - c_start[c] + j) * (H // 2) + 256 * gg + 128 * u
+                        nc.tensor.transpose(xt[:, gg, u, :], xw[:, c0:c0 + P], ident[:])
+                xt_tiles[(g, j)] = xt
+
+        def exits(g):
+            gt = SIZES[g]
+            grouped = gpool.tile([P, 2 * gt * P * 4], BF16, align_bytes=64, tag="grp", name="grouped")
+            gw = grouped[:].bitcast(F32).rearrange("p (g j r u) -> p g j r u", g=2, j=gt, u=2)
+            for j in range(gt):
+                nc.scalar.copy(out=gw[:, :, j, :, :], in_=xt_tiles[(g, j)][:].rearrange("p g u r -> p g r u"))
+            grp_tiles[g] = grouped
+
+        def quantise(g):
+            n_cols = SIZES[g] * P
+            codes = cpool.tile([P, 2 * n_cols], U32, align_bytes=64, tag="codes", name="codes")
+            scl = cpool.tile([P, 2 * n_cols], U8, align_bytes=64, tag="scl", name="scl")
+            nc.vector.quantize_mx(out=codes[:].bitcast(FP8X4), scales=scl[:], in_=grp_tiles[g][:])
+            code_tiles[g] = (codes, scl)
+
+        def mx_passes(g):
+            n_cols = SIZES[g] * P
+            codes, scl = code_tiles[g]
+            acc = acc_ps.tile([P, n_cols], F32, tag="acc", name="acc")
+            for gg in range(2):
+                nc.tensor.matmul_mx(
+                    out=acc[:],
+                    lhsT=wcodes[:, gg * P:(gg + 1) * P].bitcast(FP8X4),
+                    lhsT_scale=wscl[:, gg * P:(gg + 1) * P],
+                    rhs=codes[:, gg * n_cols:(gg + 1) * n_cols].bitcast(FP8X4),
+                    rhs_scale=scl[:, gg * n_cols:(gg + 1) * n_cols],
+                    start=(gg == 0),
+                    stop=(gg == 1),
+                )
+            acc_tiles[g] = acc
+
+        def add_bias(g):
+            ut = upool.tile([P, SIZES[g] * P], F32, tag="ut", name="ut")
+            nc.scalar.activation(out=ut[:], in_=acc_tiles[g][:], func=ACT.Identity, bias=bias32[:, 0:1], scale=1.0)
+            ut_tiles[g] = ut
+
+        def back_transposes(g):
+            up = u_ps.tile([P, SIZES[g] * P], F32, tag="up", name="up")
+            for j in range(SIZES[g]):
+                nc.tensor.transpose(up[:, j * P:(j + 1) * P], ut_tiles[g][:, j * P:(j + 1) * P], ident[:])
+            up_tiles[g] = up
+
+        def views(g):
+            c, gt = g_chunk[g], SIZES[g]
+            off = (g_start[g] - c_start[c]) * ROW
+            return s_tiles[c][:, off:off + gt * ROW], o_tiles[c][:, off:off + gt * ROW]
+
+        def seeds(g):
+            c, gt = g_chunk[g], SIZES[g]
+            if g == c_first[c]:
+                o_tiles[c] = opool.tile([P, CHUNKS[c] * ROW], F32, tag="o", name="o_sb")
+            s_g, o_g = views(g)
+            for q in range(gt * NS):
+                k = g_start[g] * NL + q * NA
+                nc.scalar.activation(
+                    out=o_g[:, q * P + CS:(q + 1) * P],
+                    in_=s_g[:, q * P:(q + 1) * P - CS],
+                    func=ACT.Copy,
+                    scale=act[:, k:k + 1],
+                )
+
+        def top_on_scalar(g):
+            s_g, o_g = views(g)
+            for q in range(SIZES[g] * NS):
+                k = g_start[g] * NL + q * NA
+                nc.scalar.activation(
+                    out=o_g[:, q * P:q * P + CS],
+                    in_=up_tiles[g][:, q * CS:(q + 1) * CS],
+                    func=ACT.Copy,
+                    scale=act[:, k:k + 1],
+                )
+
+        def top_on_vector(g):
+            t0, gt = g_start[g], SIZES[g]
+            s_g, o_g = views(g)
+            pa_bc = (
+                act[:, t0 * NL:(t0 + gt) * NL]
+                .rearrange("p (q a) -> p q a", a=NA)[:, :, 0:1]
+                .to_broadcast([P, gt * NS, CS])
+            )
+            nc.vector.tensor_tensor(
+                out=o_g.rearrange("p (q i c) -> p q i c", i=SS, c=CS)[:, :, 0, :],
+                in0=up_tiles[g][:].rearrange("p (q c) -> p q c", c=CS),
+                in1=pa_bc,
+                op=ALU.mult,
+            )
+
+        def blend(g):
+            s_g, o_g = views(g)
+            for j in range(SIZES[g]):
+                for n in range(NS):
+                    q = j * NS + n
+                    k = g_start[g] * NL + q * NA + 2
+                    nc.vector.scalar_tensor_tensor(
+                        out=o_g[:, q * P:(q + 1) * P],
+                        in0=s_g[:, q * P:(q + 1) * P],
+                        scalar=act[:, k:k + 1],
+                        in1=o_g[:, q * P:(q + 1) * P],
+                        op0=ALU.mult,
+                        op1=ALU.add,
+                    )
+                for n in range(NS):
+                    q = j * NS + n
+                    k = g_start[g] * NL + q * NA + 1
+                    nc.vector.scalar_tensor_tensor(
+                        out=o_g[:, q * P:(q + 1) * P - CS],
+                        in0=s_g[:, q * P + CS:(q + 1) * P],
+                        scalar=act[:, k:k + 1],
+                        in1=o_g[:, q * P:(q + 1) * P - CS],
+                        op0=ALU.mult,
+                        op1=ALU.add,
+                    )
+
+        def store(g):
+            c = g_chunk[g]
+            if c == n_chunks - 1:
+                s_g, o_g = views(g)
+                nc.sync.dma_start(out=out_v[:, g_start[g] * ROW:(g_start[g] + SIZES[g]) * ROW], in_=o_g)
+            elif g == c_last[c]:
+                nc.sync.dma_start(
+                    out=out_v[:, c_start[c] * ROW:(c_start[c] + CHUNKS[c]) * ROW], in_=o_tiles[c][:]
+                )
+            if g == c_last[c] and c + X_BUFS < n_chunks:
+                load(c + X_BUFS)
+
+        softmax_shift(0, HEAD_TILES)
+        softmax_exp(0, HEAD_TILES)
+        softmax_shift(HEAD_TILES, TILES)
+        softmax_norm(0, HEAD_TILES)
 
         ww = w_sb[:].bitcast(F32)
         wt = xt_ps.tile([P, 2, 2, P], F32, tag="xt", name="wt")
@@ -91,145 +280,29 @@ def tile_stackrnncore_pa_t_kernel(tc, h, act_logits, stacks, W_push, b_push, out
         bias32 = const.tile([P, 1], F32)
         nc.vector.tensor_copy(out=bias32[:], in_=b_sb[:])
 
-        mx = const.tile([P, TILES], F32)
-        dif = const.tile([P, TILES * NL], F32)
-        ex = const.tile([P, TILES * NL], F32)
-        sm = const.tile([P, TILES], F32)
-        rs = const.tile([P, TILES], F32)
-        act = const.tile([P, TILES * NL], F32)
-
-        def softmax(ta, tb):
-            n_t = tb - ta
-            cols = slice(ta * NL, tb * NL)
-            lg3 = lg[:, cols].rearrange("p (t j) -> p t j", j=NL)
-            dif3 = dif[:, cols].rearrange("p (t j) -> p t j", j=NL)
-            ex3 = ex[:, cols].rearrange("p (t j) -> p t j", j=NL)
-            act3 = act[:, cols].rearrange("p (t j) -> p t j", j=NL)
-            nc.vector.tensor_reduce(out=mx[:, ta:tb], in_=lg3, axis=AX.X, op=ALU.max)
-            nc.vector.tensor_tensor(
-                out=dif3, in0=lg3, in1=mx[:, ta:tb].unsqueeze(2).to_broadcast([P, n_t, NL]), op=ALU.subtract
-            )
-            nc.scalar.activation(out=ex[:, cols], in_=dif[:, cols], func=ACT.Exp)
-            nc.vector.tensor_reduce(out=sm[:, ta:tb], in_=ex3, axis=AX.X, op=ALU.add)
-            nc.vector.reciprocal(out=rs[:, ta:tb], in_=sm[:, ta:tb])
-            nc.vector.tensor_tensor(
-                out=act3, in0=ex3, in1=rs[:, ta:tb].unsqueeze(2).to_broadcast([P, n_t, NL]), op=ALU.mult
-            )
-
-        def stage1(g):
-            gt = SIZES[g]
-            xw = x_tiles[g][:].bitcast(F32)
-            grouped = gpool.tile([P, 2 * gt * P * 4], BF16, align_bytes=64, tag="grp", name="grouped")
-            gw = grouped[:].bitcast(F32).rearrange("p (g j r u) -> p g j r u", g=2, j=gt, u=2)
-            for j in range(gt):
-                xt = xt_ps.tile([P, 2, 2, P], F32, tag="xt", name="xt")
-                for gg in range(2):
-                    for u in range(2):
-                        c0 = j * (H // 2) + 256 * gg + 128 * u
-                        nc.tensor.transpose(xt[:, gg, u, :], xw[:, c0:c0 + P], ident[:])
-                nc.scalar.copy(out=gw[:, :, j, :, :], in_=xt[:].rearrange("p g u r -> p g r u"))
-            g_tiles[g] = grouped
-
-        def stage2(g):
-            t0, gt = starts[g], SIZES[g]
-            n_cols = gt * P
-            grouped = g_tiles[g]
-            codes = cpool.tile([P, 2 * n_cols], U32, align_bytes=64, tag="codes", name="codes")
-            scl = cpool.tile([P, 2 * n_cols], U8, align_bytes=64, tag="scl", name="scl")
-            nc.vector.quantize_mx(out=codes[:].bitcast(FP8X4), scales=scl[:], in_=grouped[:])
-            acc = acc_ps.tile([P, n_cols], F32, tag="acc", name="acc")
-            for gg in range(2):
-                nc.tensor.matmul_mx(
-                    out=acc[:],
-                    lhsT=wcodes[:, gg * P:(gg + 1) * P].bitcast(FP8X4),
-                    lhsT_scale=wscl[:, gg * P:(gg + 1) * P],
-                    rhs=codes[:, gg * n_cols:(gg + 1) * n_cols].bitcast(FP8X4),
-                    rhs_scale=scl[:, gg * n_cols:(gg + 1) * n_cols],
-                    start=(gg == 0),
-                    stop=(gg == 1),
-                )
-            ut = upool.tile([P, n_cols], F32, tag="ut", name="ut")
-            nc.scalar.activation(out=ut[:], in_=acc[:], func=ACT.Identity, bias=bias32[:, 0:1], scale=1.0)
-            up = u_ps.tile([P, n_cols], F32, tag="up", name="up")
-            for j in range(gt):
-                nc.tensor.transpose(up[:, j * P:(j + 1) * P], ut[:, j * P:(j + 1) * P], ident[:])
-            u_tiles[g] = up
-            s_sb = s_tiles[g]
-            o_sb = opool.tile([P, gt * ROW], F32, tag="o", name="o_sb")
-            o_tiles[g] = o_sb
-            for q in range(gt * NS):
-                base = q * P
-                k = t0 * NL + q * NA
-                nc.scalar.activation(
-                    out=o_sb[:, base + CS:base + P],
-                    in_=s_sb[:, base:base + P - CS],
-                    func=ACT.Copy,
-                    scale=act[:, k:k + 1],
-                )
-
-        def stage3(g):
-            t0, gt = starts[g], SIZES[g]
-            s_sb, o_sb, up = s_tiles[g], o_tiles[g], u_tiles[g]
-            if g in SCALAR_TOP:
-                for q in range(gt * NS):
-                    k = t0 * NL + q * NA
-                    nc.scalar.activation(
-                        out=o_sb[:, q * P:q * P + CS],
-                        in_=up[:, q * CS:(q + 1) * CS],
-                        func=ACT.Copy,
-                        scale=act[:, k:k + 1],
-                    )
-            else:
-                pa_bc = (
-                    act[:, t0 * NL:(t0 + gt) * NL]
-                    .rearrange("p (q a) -> p q a", a=NA)[:, :, 0:1]
-                    .to_broadcast([P, gt * NS, CS])
-                )
-                nc.vector.tensor_tensor(
-                    out=o_sb[:].rearrange("p (q i c) -> p q i c", i=SS, c=CS)[:, :, 0, :],
-                    in0=up[:].rearrange("p (q c) -> p q c", c=CS),
-                    in1=pa_bc,
-                    op=ALU.mult,
-                )
-            for j in range(gt):
-                for n in range(NS):
-                    q = j * NS + n
-                    base = q * P
-                    k = t0 * NL + q * NA + 2
-                    nc.vector.scalar_tensor_tensor(
-                        out=o_sb[:, base:base + P],
-                        in0=s_sb[:, base:base + P],
-                        scalar=act[:, k:k + 1],
-                        in1=o_sb[:, base:base + P],
-                        op0=ALU.mult,
-                        op1=ALU.add,
-                    )
-                for n in range(NS):
-                    q = j * NS + n
-                    base = q * P
-                    k = t0 * NL + q * NA + 1
-                    nc.vector.scalar_tensor_tensor(
-                        out=o_sb[:, base:base + P - CS],
-                        in0=s_sb[:, base + CS:base + P],
-                        scalar=act[:, k:k + 1],
-                        in1=o_sb[:, base:base + P - CS],
-                        op0=ALU.mult,
-                        op1=ALU.add,
-                    )
-            nc.sync.dma_start(out=out_v[:, t0 * ROW:(t0 + gt) * ROW], in_=o_sb[:])
-
-        softmax(0, HEAD_TILES)
-        stage1(0)
-        load(2)
-        stage2(0)
-        stage1(1)
-        load(3)
-        softmax(HEAD_TILES, TILES)
-        for g in range(n_groups):
-            if g + 4 < n_groups:
-                load(g + 4)
-            if g + 1 < n_groups:
-                stage2(g + 1)
-            if g + 2 < n_groups:
-                stage1(g + 2)
-            stage3(g)
+        for k in range(-3, n_groups):
+            if k >= 1:
+                store(k - 1)
+            if k + 3 < n_groups:
+                transposes(k + 3)
+            if 0 <= k + 1 < n_groups:
+                add_bias(k + 1)
+                back_transposes(k + 1)
+            if k >= 0 and not scalar_top(k):
+                top_on_vector(k)
+            if 0 <= k + 2 < n_groups:
+                quantise(k + 2)
+                mx_passes(k + 2)
+            if k == -2:
+                softmax_exp(HEAD_TILES, TILES)
+            if k == -1:
+                softmax_norm(HEAD_TILES, TILES)
+            if 0 <= k + 1 < n_groups:
+                seeds(k + 1)
+            if k + 3 < n_groups:
+                exits(k + 3)
+            if 0 <= k + 1 < n_groups and scalar_top(k + 1):
+                top_on_scalar(k + 1)
+            if k >= 0:
+                blend(k)
+        store(n_groups - 1)

@@ -43,7 +43,7 @@ def tile_stackrnncore_pa_t_kernel(tc, h, act_logits, stacks, W_push, b_push, out
     c_first = [min(g for g in range(n_groups) if g_chunk[g] == c) for c in range(n_chunks)]
 
     def scalar_top(g):
-        return g % 3 != 0
+        return (g >= 7 and g % 4 != 0) or g > n_groups - 7
 
     with ExitStack() as ctx:
         const = ctx.enter_context(tc.tile_pool(name="const", bufs=1))
@@ -100,8 +100,10 @@ def tile_stackrnncore_pa_t_kernel(tc, h, act_logits, stacks, W_push, b_push, out
         def by_row(t, ta, tb):
             return t[:, ta * NL:tb * NL].rearrange("p (t j) -> p t j", j=NL)
 
-        def softmax_shift(ta, tb):
+        def softmax_max(ta, tb):
             nc.vector.tensor_reduce(out=mx[:, ta:tb], in_=by_row(lg, ta, tb), axis=AX.X, op=ALU.max)
+
+        def softmax_shift(ta, tb):
             nc.vector.tensor_tensor(
                 out=by_row(dif, ta, tb),
                 in0=by_row(lg, ta, tb),
@@ -258,10 +260,12 @@ def tile_stackrnncore_pa_t_kernel(tc, h, act_logits, stacks, W_push, b_push, out
             if g == c_last[c] and c + X_BUFS < n_chunks:
                 load(c + X_BUFS)
 
+        softmax_max(0, HEAD_TILES)
         softmax_shift(0, HEAD_TILES)
         softmax_exp(0, HEAD_TILES)
-        softmax_shift(HEAD_TILES, TILES)
+        softmax_max(HEAD_TILES, TILES)
         softmax_norm(0, HEAD_TILES)
+        softmax_shift(HEAD_TILES, TILES)
 
         ww = w_sb[:].bitcast(F32)
         wt = xt_ps.tile([P, 2, 2, P], F32, tag="xt", name="wt")

@@ -43,7 +43,7 @@ def tile_stackrnncore_pa_t_kernel(tc, h, act_logits, stacks, W_push, b_push, out
     c_first = [min(g for g in range(n_groups) if g_chunk[g] == c) for c in range(n_chunks)]
 
     def scalar_top(g):
-        return (g >= 7 and g % 4 != 0) or g > n_groups - 7
+        return g >= 4
 
     with ExitStack() as ctx:
         const = ctx.enter_context(tc.tile_pool(name="const", bufs=1))

@@ -14,17 +14,19 @@ AX = mybir.AxisListType
 
 P = 128
 B, H, NS, SS, CS, NA = 6144, 1024, 4, 4, 32, 3
-NC = NS * CS
-ROW = NS * SS * CS
-TILES = B // P
+STACK = SS * CS
+ROW = NS * STACK
 NL = NS * NA
-FLOPS = 2 * B * H * NC
+TILES = B // P
+PACK = 4
+PASSES = H // (P * PACK)
+WORDS = H // 2
+FLOPS = 2 * B * H * P
 
 SIZES = [1, 1, 1, 1] + [2] * 21 + [1, 1]
 CHUNKS = [1, 1, 2] + [4] * 11
 HEAD_TILES = 4
-X_BUFS = 6
-S_BUFS = 8
+LOAD_BUFS = 6
 O_BUFS = 5
 
 
@@ -34,28 +36,26 @@ def tile_stackrnncore_pa_t_kernel(tc, h, act_logits, stacks, W_push, b_push, out
     st_v = stacks.rearrange("(p t) n i c -> p (t n i c)", t=TILES)
     out_v = out.rearrange("(p t) n i c -> p (t n i c)", t=TILES)
     lg_v = act_logits.rearrange("(p t) j -> p (t j)", t=TILES)
+
     n_groups = len(SIZES)
     n_chunks = len(CHUNKS)
     g_start = [sum(SIZES[:g]) for g in range(n_groups)]
     c_start = [sum(CHUNKS[:c]) for c in range(n_chunks)]
     g_chunk = [max(c for c in range(n_chunks) if c_start[c] <= g_start[g]) for g in range(n_groups)]
-    c_last = [max(g for g in range(n_groups) if g_chunk[g] == c) for c in range(n_chunks)]
     c_first = [min(g for g in range(n_groups) if g_chunk[g] == c) for c in range(n_chunks)]
-
-    def scalar_top(g):
-        return g >= 4
+    c_last = [max(g for g in range(n_groups) if g_chunk[g] == c) for c in range(n_chunks)]
 
     with ExitStack() as ctx:
         const = ctx.enter_context(tc.tile_pool(name="const", bufs=1))
-        hpool = ctx.enter_context(tc.tile_pool(name="hpool", bufs=X_BUFS))
-        spool = ctx.enter_context(tc.tile_pool(name="spool", bufs=S_BUFS))
+        hpool = ctx.enter_context(tc.tile_pool(name="hpool", bufs=LOAD_BUFS))
+        spool = ctx.enter_context(tc.tile_pool(name="spool", bufs=LOAD_BUFS))
+        opool = ctx.enter_context(tc.tile_pool(name="opool", bufs=O_BUFS))
         gpool = ctx.enter_context(tc.tile_pool(name="gpool", bufs=2))
         cpool = ctx.enter_context(tc.tile_pool(name="cpool", bufs=2))
         upool = ctx.enter_context(tc.tile_pool(name="upool", bufs=2))
-        opool = ctx.enter_context(tc.tile_pool(name="opool", bufs=O_BUFS))
         xt_ps = ctx.enter_context(tc.psum_pool(name="xt_ps", bufs=4))
         acc_ps = ctx.enter_context(tc.psum_pool(name="acc_ps", bufs=2))
-        u_ps = ctx.enter_context(tc.psum_pool(name="u_ps", bufs=2))
+        push_ps = ctx.enter_context(tc.psum_pool(name="push_ps", bufs=2))
         ctx.enter_context(tc.manual_schedule())
 
         x_tiles = {}
@@ -65,11 +65,11 @@ def tile_stackrnncore_pa_t_kernel(tc, h, act_logits, stacks, W_push, b_push, out
         grp_tiles = {}
         code_tiles = {}
         acc_tiles = {}
-        ut_tiles = {}
-        up_tiles = {}
+        sum_tiles = {}
+        push_tiles = {}
 
-        lg = const.tile([P, TILES * NL], BF16)
-        nc.sync.dma_start(out=lg[:], in_=lg_v)
+        logits = const.tile([P, TILES * NL], BF16)
+        nc.sync.dma_start(out=logits[:], in_=lg_v)
         w_sb = const.tile([P, H], BF16)
         nc.sync.dma_start(out=w_sb[:], in_=W_push)
         b_sb = const.tile([P, 1], BF16)
@@ -84,181 +84,152 @@ def tile_stackrnncore_pa_t_kernel(tc, h, act_logits, stacks, W_push, b_push, out
             x_tiles[c] = x_sb
             s_tiles[c] = s_sb
 
-        for c in range(X_BUFS):
+        for c in range(LOAD_BUFS):
             load(c)
 
         ident = const.tile([P, P], F32)
         make_identity(nc, ident[:])
 
-        mx = const.tile([P, TILES], F32)
-        dif = const.tile([P, TILES * NL], F32)
-        ex = const.tile([P, TILES * NL], F32)
-        sm = const.tile([P, TILES], F32)
-        rs = const.tile([P, TILES], F32)
+        row_max = const.tile([P, TILES], F32)
+        shifted = const.tile([P, TILES * NL], F32)
+        expd = const.tile([P, TILES * NL], F32)
+        row_sum = const.tile([P, TILES], F32)
+        row_inv = const.tile([P, TILES], F32)
         act = const.tile([P, TILES * NL], F32)
 
-        def by_row(t, ta, tb):
-            return t[:, ta * NL:tb * NL].rearrange("p (t j) -> p t j", j=NL)
+        def by_row(values, ta, tb):
+            return values[:, ta * NL:tb * NL].rearrange("p (t j) -> p t j", j=NL)
+
+        def per_row(values, ta, tb):
+            return values[:, ta:tb].unsqueeze(2).to_broadcast([P, tb - ta, NL])
 
         def softmax_max(ta, tb):
-            nc.vector.tensor_reduce(out=mx[:, ta:tb], in_=by_row(lg, ta, tb), axis=AX.X, op=ALU.max)
+            nc.vector.tensor_reduce(out=row_max[:, ta:tb], in_=by_row(logits, ta, tb), axis=AX.X, op=ALU.max)
 
         def softmax_shift(ta, tb):
             nc.vector.tensor_tensor(
-                out=by_row(dif, ta, tb),
-                in0=by_row(lg, ta, tb),
-                in1=mx[:, ta:tb].unsqueeze(2).to_broadcast([P, tb - ta, NL]),
-                op=ALU.subtract,
+                out=by_row(shifted, ta, tb), in0=by_row(logits, ta, tb), in1=per_row(row_max, ta, tb), op=ALU.subtract
             )
 
         def softmax_exp(ta, tb):
-            nc.scalar.activation(out=ex[:, ta * NL:tb * NL], in_=dif[:, ta * NL:tb * NL], func=ACT.Exp)
+            nc.scalar.activation(out=expd[:, ta * NL:tb * NL], in_=shifted[:, ta * NL:tb * NL], func=ACT.Exp)
 
         def softmax_norm(ta, tb):
-            nc.vector.tensor_reduce(out=sm[:, ta:tb], in_=by_row(ex, ta, tb), axis=AX.X, op=ALU.add)
-            nc.vector.reciprocal(out=rs[:, ta:tb], in_=sm[:, ta:tb])
+            nc.vector.tensor_reduce(out=row_sum[:, ta:tb], in_=by_row(expd, ta, tb), axis=AX.X, op=ALU.add)
+            nc.vector.reciprocal(out=row_inv[:, ta:tb], in_=row_sum[:, ta:tb])
             nc.vector.tensor_tensor(
-                out=by_row(act, ta, tb),
-                in0=by_row(ex, ta, tb),
-                in1=rs[:, ta:tb].unsqueeze(2).to_broadcast([P, tb - ta, NL]),
-                op=ALU.mult,
+                out=by_row(act, ta, tb), in0=by_row(expd, ta, tb), in1=per_row(row_inv, ta, tb), op=ALU.mult
             )
 
-        def transposes(g):
-            c, gt = g_chunk[g], SIZES[g]
-            xw = x_tiles[c][:].bitcast(F32)
-            for j in range(gt):
-                xt = xt_ps.tile([P, 2, 2, P], F32, tag="xt", name="xt")
-                for gg in range(2):
-                    for u in range(2):
-                        c0 = (g_start[g] - c_start[c] + j) * (H // 2) + 256 * gg + 128 * u
-                        nc.tensor.transpose(xt[:, gg, u, :], xw[:, c0:c0 + P], ident[:])
-                xt_tiles[(g, j)] = xt
+        def transpose_words(words, first_word):
+            xt = xt_ps.tile([P, PASSES, 2, P], F32, tag="xt", name="xt")
+            for m in range(PASSES):
+                for u in range(2):
+                    w0 = first_word + (2 * m + u) * P
+                    nc.tensor.transpose(xt[:, m, u, :], words[:, w0:w0 + P], ident[:])
+            return xt
 
-        def exits(g):
+        def copy_out(xt, grouped_words):
+            nc.scalar.copy(out=grouped_words, in_=xt[:].rearrange("p m u r -> p m r u"))
+
+        def transposes(g):
+            c = g_chunk[g]
+            words = x_tiles[c][:].bitcast(F32)
+            for j in range(SIZES[g]):
+                xt_tiles[(g, j)] = transpose_words(words, (g_start[g] - c_start[c] + j) * WORDS)
+
+        def copies_out(g):
             gt = SIZES[g]
-            grouped = gpool.tile([P, 2 * gt * P * 4], BF16, align_bytes=64, tag="grp", name="grouped")
-            gw = grouped[:].bitcast(F32).rearrange("p (g j r u) -> p g j r u", g=2, j=gt, u=2)
+            grouped = gpool.tile([P, PASSES * gt * P * PACK], BF16, align_bytes=64, tag="grp", name="grouped")
+            gw = grouped[:].bitcast(F32).rearrange("p (m j r u) -> p m j r u", m=PASSES, j=gt, u=2)
             for j in range(gt):
-                nc.scalar.copy(out=gw[:, :, j, :, :], in_=xt_tiles[(g, j)][:].rearrange("p g u r -> p g r u"))
+                copy_out(xt_tiles[(g, j)], gw[:, :, j, :, :])
             grp_tiles[g] = grouped
 
         def quantise(g):
             n_cols = SIZES[g] * P
-            codes = cpool.tile([P, 2 * n_cols], U32, align_bytes=64, tag="codes", name="codes")
-            scl = cpool.tile([P, 2 * n_cols], U8, align_bytes=64, tag="scl", name="scl")
-            nc.vector.quantize_mx(out=codes[:].bitcast(FP8X4), scales=scl[:], in_=grp_tiles[g][:])
-            code_tiles[g] = (codes, scl)
+            codes = cpool.tile([P, PASSES * n_cols], U32, align_bytes=64, tag="codes", name="codes")
+            scales = cpool.tile([P, PASSES * n_cols], U8, align_bytes=64, tag="scales", name="scales")
+            nc.vector.quantize_mx(out=codes[:].bitcast(FP8X4), scales=scales[:], in_=grp_tiles[g][:])
+            code_tiles[g] = (codes, scales)
 
         def mx_passes(g):
             n_cols = SIZES[g] * P
-            codes, scl = code_tiles[g]
+            codes, scales = code_tiles[g]
             acc = acc_ps.tile([P, n_cols], F32, tag="acc", name="acc")
-            for gg in range(2):
+            for m in range(PASSES):
                 nc.tensor.matmul_mx(
                     out=acc[:],
-                    lhsT=wcodes[:, gg * P:(gg + 1) * P].bitcast(FP8X4),
-                    lhsT_scale=wscl[:, gg * P:(gg + 1) * P],
-                    rhs=codes[:, gg * n_cols:(gg + 1) * n_cols].bitcast(FP8X4),
-                    rhs_scale=scl[:, gg * n_cols:(gg + 1) * n_cols],
-                    start=(gg == 0),
-                    stop=(gg == 1),
+                    lhsT=w_codes[:, m * P:(m + 1) * P].bitcast(FP8X4),
+                    lhsT_scale=w_scales[:, m * P:(m + 1) * P],
+                    rhs=codes[:, m * n_cols:(m + 1) * n_cols].bitcast(FP8X4),
+                    rhs_scale=scales[:, m * n_cols:(m + 1) * n_cols],
+                    start=(m == 0),
+                    stop=(m == PASSES - 1),
                 )
             acc_tiles[g] = acc
 
         def add_bias(g):
-            ut = upool.tile([P, SIZES[g] * P], F32, tag="ut", name="ut")
-            nc.scalar.activation(out=ut[:], in_=acc_tiles[g][:], func=ACT.Identity, bias=bias32[:, 0:1], scale=1.0)
-            ut_tiles[g] = ut
+            sums = upool.tile([P, SIZES[g] * P], F32, tag="sums", name="sums")
+            nc.scalar.activation(out=sums[:], in_=acc_tiles[g][:], func=ACT.Identity, bias=bias[:, 0:1], scale=1.0)
+            sum_tiles[g] = sums
 
         def back_transposes(g):
-            up = u_ps.tile([P, SIZES[g] * P], F32, tag="up", name="up")
+            push = push_ps.tile([P, SIZES[g] * P], F32, tag="push", name="push")
             for j in range(SIZES[g]):
-                nc.tensor.transpose(up[:, j * P:(j + 1) * P], ut_tiles[g][:, j * P:(j + 1) * P], ident[:])
-            up_tiles[g] = up
+                nc.tensor.transpose(push[:, j * P:(j + 1) * P], sum_tiles[g][:, j * P:(j + 1) * P], ident[:])
+            push_tiles[g] = push
 
-        def views(g):
-            c, gt = g_chunk[g], SIZES[g]
-            off = (g_start[g] - c_start[c]) * ROW
-            return s_tiles[c][:, off:off + gt * ROW], o_tiles[c][:, off:off + gt * ROW]
+        def stacks_of(g):
+            c = g_chunk[g]
+            entries = []
+            for q in range(SIZES[g] * NS):
+                lo = (g_start[g] - c_start[c]) * ROW + q * STACK
+                entries.append((q, s_tiles[c][:, lo:lo + STACK], o_tiles[c][:, lo:lo + STACK], g_start[g] * NL + q * NA))
+            return entries
 
-        def seeds(g):
-            c, gt = g_chunk[g], SIZES[g]
+        def seed_lower_cells(g):
+            c = g_chunk[g]
             if g == c_first[c]:
                 o_tiles[c] = opool.tile([P, CHUNKS[c] * ROW], F32, tag="o", name="o_sb")
-            s_g, o_g = views(g)
-            for q in range(gt * NS):
-                k = g_start[g] * NL + q * NA
+            for q, s_q, o_q, a_q in stacks_of(g):
                 nc.scalar.activation(
-                    out=o_g[:, q * P + CS:(q + 1) * P],
-                    in_=s_g[:, q * P:(q + 1) * P - CS],
-                    func=ACT.Copy,
-                    scale=act[:, k:k + 1],
+                    out=o_q[:, CS:STACK], in_=s_q[:, 0:STACK - CS], func=ACT.Copy, scale=act[:, a_q:a_q + 1]
                 )
 
-        def top_on_scalar(g):
-            s_g, o_g = views(g)
-            for q in range(SIZES[g] * NS):
-                k = g_start[g] * NL + q * NA
+        def seed_top_cells(g):
+            for q, s_q, o_q, a_q in stacks_of(g):
                 nc.scalar.activation(
-                    out=o_g[:, q * P:q * P + CS],
-                    in_=up_tiles[g][:, q * CS:(q + 1) * CS],
-                    func=ACT.Copy,
-                    scale=act[:, k:k + 1],
+                    out=o_q[:, 0:CS], in_=push_tiles[g][:, q * CS:(q + 1) * CS], func=ACT.Copy, scale=act[:, a_q:a_q + 1]
                 )
-
-        def top_on_vector(g):
-            t0, gt = g_start[g], SIZES[g]
-            s_g, o_g = views(g)
-            pa_bc = (
-                act[:, t0 * NL:(t0 + gt) * NL]
-                .rearrange("p (q a) -> p q a", a=NA)[:, :, 0:1]
-                .to_broadcast([P, gt * NS, CS])
-            )
-            nc.vector.tensor_tensor(
-                out=o_g.rearrange("p (q i c) -> p q i c", i=SS, c=CS)[:, :, 0, :],
-                in0=up_tiles[g][:].rearrange("p (q c) -> p q c", c=CS),
-                in1=pa_bc,
-                op=ALU.mult,
-            )
 
         def blend(g):
-            s_g, o_g = views(g)
+            entries = stacks_of(g)
             for j in range(SIZES[g]):
-                for n in range(NS):
-                    q = j * NS + n
-                    k = g_start[g] * NL + q * NA + 2
+                for q, s_q, o_q, a_q in entries[j * NS:(j + 1) * NS]:
                     nc.vector.scalar_tensor_tensor(
-                        out=o_g[:, q * P:(q + 1) * P],
-                        in0=s_g[:, q * P:(q + 1) * P],
-                        scalar=act[:, k:k + 1],
-                        in1=o_g[:, q * P:(q + 1) * P],
-                        op0=ALU.mult,
-                        op1=ALU.add,
+                        out=o_q, in0=s_q, scalar=act[:, a_q + 2:a_q + 3], in1=o_q, op0=ALU.mult, op1=ALU.add
                     )
-                for n in range(NS):
-                    q = j * NS + n
-                    k = g_start[g] * NL + q * NA + 1
+                for q, s_q, o_q, a_q in entries[j * NS:(j + 1) * NS]:
                     nc.vector.scalar_tensor_tensor(
-                        out=o_g[:, q * P:(q + 1) * P - CS],
-                        in0=s_g[:, q * P + CS:(q + 1) * P],
-                        scalar=act[:, k:k + 1],
-                        in1=o_g[:, q * P:(q + 1) * P - CS],
+                        out=o_q[:, 0:STACK - CS],
+                        in0=s_q[:, CS:STACK],
+                        scalar=act[:, a_q + 1:a_q + 2],
+                        in1=o_q[:, 0:STACK - CS],
                         op0=ALU.mult,
                         op1=ALU.add,
                     )
 
         def store(g):
             c = g_chunk[g]
+            t0, gt = g_start[g], SIZES[g]
             if c == n_chunks - 1:
-                s_g, o_g = views(g)
-                nc.sync.dma_start(out=out_v[:, g_start[g] * ROW:(g_start[g] + SIZES[g]) * ROW], in_=o_g)
+                lo = (t0 - c_start[c]) * ROW
+                nc.sync.dma_start(out=out_v[:, t0 * ROW:(t0 + gt) * ROW], in_=o_tiles[c][:, lo:lo + gt * ROW])
             elif g == c_last[c]:
-                nc.sync.dma_start(
-                    out=out_v[:, c_start[c] * ROW:(c_start[c] + CHUNKS[c]) * ROW], in_=o_tiles[c][:]
-                )
-            if g == c_last[c] and c + X_BUFS < n_chunks:
-                load(c + X_BUFS)
+                nc.sync.dma_start(out=out_v[:, c_start[c] * ROW:(c_start[c] + CHUNKS[c]) * ROW], in_=o_tiles[c][:])
+            if g == c_last[c] and c + LOAD_BUFS < n_chunks:
+                load(c + LOAD_BUFS)
 
         softmax_max(0, HEAD_TILES)
         softmax_shift(0, HEAD_TILES)
@@ -267,22 +238,16 @@ def tile_stackrnncore_pa_t_kernel(tc, h, act_logits, stacks, W_push, b_push, out
         softmax_norm(0, HEAD_TILES)
         softmax_shift(HEAD_TILES, TILES)
 
-        ww = w_sb[:].bitcast(F32)
-        wt = xt_ps.tile([P, 2, 2, P], F32, tag="xt", name="wt")
-        for gg in range(2):
-            for u in range(2):
-                c0 = 256 * gg + 128 * u
-                nc.tensor.transpose(wt[:, gg, u, :], ww[:, c0:c0 + P], ident[:])
-        wgrouped = const.tile([P, 2 * P * 4], BF16, align_bytes=64)
-        nc.scalar.copy(
-            out=wgrouped[:].bitcast(F32).rearrange("p (g r u) -> p g r u", g=2, u=2),
-            in_=wt[:].rearrange("p g u r -> p g r u"),
+        w_grouped = const.tile([P, PASSES * P * PACK], BF16, align_bytes=64)
+        copy_out(
+            transpose_words(w_sb[:].bitcast(F32), 0),
+            w_grouped[:].bitcast(F32).rearrange("p (m r u) -> p m r u", m=PASSES, u=2),
         )
-        wcodes = const.tile([P, 2 * P], U32, align_bytes=64)
-        wscl = const.tile([P, 2 * P], U8, align_bytes=64)
-        nc.vector.quantize_mx(out=wcodes[:].bitcast(FP8X4), scales=wscl[:], in_=wgrouped[:])
-        bias32 = const.tile([P, 1], F32)
-        nc.vector.tensor_copy(out=bias32[:], in_=b_sb[:])
+        w_codes = const.tile([P, PASSES * P], U32, align_bytes=64)
+        w_scales = const.tile([P, PASSES * P], U8, align_bytes=64)
+        nc.vector.quantize_mx(out=w_codes[:].bitcast(FP8X4), scales=w_scales[:], in_=w_grouped[:])
+        bias = const.tile([P, 1], F32)
+        nc.vector.tensor_copy(out=bias[:], in_=b_sb[:])
 
         for k in range(-3, n_groups):
             if k >= 1:
@@ -292,8 +257,6 @@ def tile_stackrnncore_pa_t_kernel(tc, h, act_logits, stacks, W_push, b_push, out
             if 0 <= k + 1 < n_groups:
                 add_bias(k + 1)
                 back_transposes(k + 1)
-            if k >= 0 and not scalar_top(k):
-                top_on_vector(k)
             if 0 <= k + 2 < n_groups:
                 quantise(k + 2)
                 mx_passes(k + 2)
@@ -302,11 +265,11 @@ def tile_stackrnncore_pa_t_kernel(tc, h, act_logits, stacks, W_push, b_push, out
             if k == -1:
                 softmax_norm(HEAD_TILES, TILES)
             if 0 <= k + 1 < n_groups:
-                seeds(k + 1)
+                seed_lower_cells(k + 1)
             if k + 3 < n_groups:
-                exits(k + 3)
-            if 0 <= k + 1 < n_groups and scalar_top(k + 1):
-                top_on_scalar(k + 1)
+                copies_out(k + 3)
+            if 0 <= k + 1 < n_groups:
+                seed_top_cells(k + 1)
             if k >= 0:
                 blend(k)
         store(n_groups - 1)

from contextlib import ExitStack

import concourse.mybir as mybir
from concourse.masks import make_identity

F32 = mybir.dt.float32
BF16 = mybir.dt.bfloat16
U32 = mybir.dt.uint32
U8 = mybir.dt.uint8
FP8X4 = mybir.dt.float8_e4m3fn_x4
ALU = mybir.AluOpType
ACT = mybir.ActivationFunctionType
AX = mybir.AxisListType

P = 128
B, H, NS, SS, CS, NA = 6144, 1024, 4, 4, 32, 3
STACK = SS * CS
ROW = NS * STACK
NL = NS * NA
TILES = B // P
PACK = 4
PASSES = H // (P * PACK)
WORDS = H // 2
FLOPS = 2 * B * H * P

SIZES = [1, 1, 1, 1] + [2] * 21 + [1, 1]
CHUNKS = [1, 1, 2] + [4] * 11
HEAD_TILES = 4
LOAD_BUFS = 6
O_BUFS = 5


def tile_stackrnncore_pa_t_kernel(tc, h, act_logits, stacks, W_push, b_push, out):
    nc = tc.nc
    h_v = h.rearrange("(p t) k -> p (t k)", t=TILES)
    st_v = stacks.rearrange("(p t) n i c -> p (t n i c)", t=TILES)
    out_v = out.rearrange("(p t) n i c -> p (t n i c)", t=TILES)
    lg_v = act_logits.rearrange("(p t) j -> p (t j)", t=TILES)

    n_groups = len(SIZES)
    n_chunks = len(CHUNKS)
    g_start = [sum(SIZES[:g]) for g in range(n_groups)]
    c_start = [sum(CHUNKS[:c]) for c in range(n_chunks)]
    g_chunk = [max(c for c in range(n_chunks) if c_start[c] <= g_start[g]) for g in range(n_groups)]
    c_first = [min(g for g in range(n_groups) if g_chunk[g] == c) for c in range(n_chunks)]
    c_last = [max(g for g in range(n_groups) if g_chunk[g] == c) for c in range(n_chunks)]

    with ExitStack() as ctx:
        const = ctx.enter_context(tc.tile_pool(name="const", bufs=1))
        hpool = ctx.enter_context(tc.tile_pool(name="hpool", bufs=LOAD_BUFS))
        spool = ctx.enter_context(tc.tile_pool(name="spool", bufs=LOAD_BUFS))
        opool = ctx.enter_context(tc.tile_pool(name="opool", bufs=O_BUFS))
        gpool = ctx.enter_context(tc.tile_pool(name="gpool", bufs=2))
        cpool = ctx.enter_context(tc.tile_pool(name="cpool", bufs=2))
        upool = ctx.enter_context(tc.tile_pool(name="upool", bufs=2))
        xt_ps = ctx.enter_context(tc.psum_pool(name="xt_ps", bufs=4))
        acc_ps = ctx.enter_context(tc.psum_pool(name="acc_ps", bufs=2))
        push_ps = ctx.enter_context(tc.psum_pool(name="push_ps", bufs=2))
        ctx.enter_context(tc.manual_schedule())

        x_tiles = {}
        s_tiles = {}
        o_tiles = {}
        xt_tiles = {}
        grp_tiles = {}
        code_tiles = {}
        acc_tiles = {}
        sum_tiles = {}
        push_tiles = {}

        logits = const.tile([P, TILES * NL], BF16)
        nc.sync.dma_start(out=logits[:], in_=lg_v)
        w_sb = const.tile([P, H], BF16)
        nc.sync.dma_start(out=w_sb[:], in_=W_push)
        b_sb = const.tile([P, 1], BF16)
        nc.sync.dma_start(out=b_sb[:], in_=b_push.rearrange("(p o) -> p o", o=1))

        def load(c):
            t0, ct = c_start[c], CHUNKS[c]
            x_sb = hpool.tile([P, ct * H], BF16, tag="x", name="x_sb")
            nc.sync.dma_start(out=x_sb[:], in_=h_v[:, t0 * H:(t0 + ct) * H])
            s_sb = spool.tile([P, ct * ROW], BF16, tag="s", name="s_sb")
            nc.sync.dma_start(out=s_sb[:], in_=st_v[:, t0 * ROW:(t0 + ct) * ROW])
            x_tiles[c] = x_sb
            s_tiles[c] = s_sb

        for c in range(LOAD_BUFS):
            load(c)

        ident = const.tile([P, P], F32)
        make_identity(nc, ident[:])

        row_max = const.tile([P, TILES], F32)
        shifted = const.tile([P, TILES * NL], F32)
        expd = const.tile([P, TILES * NL], F32)
        row_sum = const.tile([P, TILES], F32)
        row_inv = const.tile([P, TILES], F32)
        act = const.tile([P, TILES * NL], F32)

        def by_row(values, ta, tb):
            return values[:, ta * NL:tb * NL].rearrange("p (t j) -> p t j", j=NL)

        def per_row(values, ta, tb):
            return values[:, ta:tb].unsqueeze(2).to_broadcast([P, tb - ta, NL])

        def softmax_max(ta, tb):
            nc.vector.tensor_reduce(out=row_max[:, ta:tb], in_=by_row(logits, ta, tb), axis=AX.X, op=ALU.max)

        def softmax_shift(ta, tb):
            nc.vector.tensor_tensor(
                out=by_row(shifted, ta, tb), in0=by_row(logits, ta, tb), in1=per_row(row_max, ta, tb), op=ALU.subtract
            )

        def softmax_exp(ta, tb):
            nc.scalar.activation(out=expd[:, ta * NL:tb * NL], in_=shifted[:, ta * NL:tb * NL], func=ACT.Exp)

        def softmax_norm(ta, tb):
            nc.vector.tensor_reduce(out=row_sum[:, ta:tb], in_=by_row(expd, ta, tb), axis=AX.X, op=ALU.add)
            nc.vector.reciprocal(out=row_inv[:, ta:tb], in_=row_sum[:, ta:tb])
            nc.vector.tensor_tensor(
                out=by_row(act, ta, tb), in0=by_row(expd, ta, tb), in1=per_row(row_inv, ta, tb), op=ALU.mult
            )

        def transpose_words(words, first_word):
            xt = xt_ps.tile([P, PASSES, 2, P], F32, tag="xt", name="xt")
            for m in range(PASSES):
                for u in range(2):
                    w0 = first_word + (2 * m + u) * P
                    nc.tensor.transpose(xt[:, m, u, :], words[:, w0:w0 + P], ident[:])
            return xt

        def copy_out(xt, grouped_words):
            nc.scalar.copy(out=grouped_words, in_=xt[:].rearrange("p m u r -> p m r u"))

        def transposes(g):
            c = g_chunk[g]
            words = x_tiles[c][:].bitcast(F32)
            for j in range(SIZES[g]):
                xt_tiles[(g, j)] = transpose_words(words, (g_start[g] - c_start[c] + j) * WORDS)

        def copies_out(g):
            gt = SIZES[g]
            grouped = gpool.tile([P, PASSES * gt * P * PACK], BF16, align_bytes=64, tag="grp", name="grouped")
            gw = grouped[:].bitcast(F32).rearrange("p (m j r u) -> p m j r u", m=PASSES, j=gt, u=2)
            for j in range(gt):
                copy_out(xt_tiles[(g, j)], gw[:, :, j, :, :])
            grp_tiles[g] = grouped

        def quantise(g):
            n_cols = SIZES[g] * P
            codes = cpool.tile([P, PASSES * n_cols], U32, align_bytes=64, tag="codes", name="codes")
            scales = cpool.tile([P, PASSES * n_cols], U8, align_bytes=64, tag="scales", name="scales")
            nc.vector.quantize_mx(out=codes[:].bitcast(FP8X4), scales=scales[:], in_=grp_tiles[g][:])
            code_tiles[g] = (codes, scales)

        def mx_passes(g):
            n_cols = SIZES[g] * P
            codes, scales = code_tiles[g]
            acc = acc_ps.tile([P, n_cols], F32, tag="acc", name="acc")
            for m in range(PASSES):
                nc.tensor.matmul_mx(
                    out=acc[:],
                    lhsT=w_codes[:, m * P:(m + 1) * P].bitcast(FP8X4),
                    lhsT_scale=w_scales[:, m * P:(m + 1) * P],
                    rhs=codes[:, m * n_cols:(m + 1) * n_cols].bitcast(FP8X4),
                    rhs_scale=scales[:, m * n_cols:(m + 1) * n_cols],
                    start=(m == 0),
                    stop=(m == PASSES - 1),
                )
            acc_tiles[g] = acc

        def add_bias(g):
            sums = upool.tile([P, SIZES[g] * P], F32, tag="sums", name="sums")
            nc.scalar.activation(out=sums[:], in_=acc_tiles[g][:], func=ACT.Identity, bias=bias[:, 0:1], scale=1.0)
            sum_tiles[g] = sums

        def back_transposes(g):
            push = push_ps.tile([P, SIZES[g] * P], F32, tag="push", name="push")
            for j in range(SIZES[g]):
                nc.tensor.transpose(push[:, j * P:(j + 1) * P], sum_tiles[g][:, j * P:(j + 1) * P], ident[:])
            push_tiles[g] = push

        def stacks_of(g):
            c = g_chunk[g]
            entries = []
            for q in range(SIZES[g] * NS):
                lo = (g_start[g] - c_start[c]) * ROW + q * STACK
                entries.append((q, s_tiles[c][:, lo:lo + STACK], o_tiles[c][:, lo:lo + STACK], g_start[g] * NL + q * NA))
            return entries

        def seed_lower_cells(g):
            c = g_chunk[g]
            if g == c_first[c]:
                o_tiles[c] = opool.tile([P, CHUNKS[c] * ROW], F32, tag="o", name="o_sb")
            for q, s_q, o_q, a_q in stacks_of(g):
                nc.scalar.activation(
                    out=o_q[:, CS:STACK], in_=s_q[:, 0:STACK - CS], func=ACT.Copy, scale=act[:, a_q:a_q + 1]
                )

        def seed_top_cells(g):
            for q, s_q, o_q, a_q in stacks_of(g):
                nc.scalar.activation(
                    out=o_q[:, 0:CS], in_=push_tiles[g][:, q * CS:(q + 1) * CS], func=ACT.Copy, scale=act[:, a_q:a_q + 1]
                )

        def blend(g):
            entries = stacks_of(g)
            for j in range(SIZES[g]):
                for q, s_q, o_q, a_q in entries[j * NS:(j + 1) * NS]:
                    nc.vector.scalar_tensor_tensor(
                        out=o_q, in0=s_q, scalar=act[:, a_q + 2:a_q + 3], in1=o_q, op0=ALU.mult, op1=ALU.add
                    )
                for q, s_q, o_q, a_q in entries[j * NS:(j + 1) * NS]:
                    nc.vector.scalar_tensor_tensor(
                        out=o_q[:, 0:STACK - CS],
                        in0=s_q[:, CS:STACK],
                        scalar=act[:, a_q + 1:a_q + 2],
                        in1=o_q[:, 0:STACK - CS],
                        op0=ALU.mult,
                        op1=ALU.add,
                    )

        def store(g):
            c = g_chunk[g]
            t0, gt = g_start[g], SIZES[g]
            if c == n_chunks - 1:
                lo = (t0 - c_start[c]) * ROW
                nc.sync.dma_start(out=out_v[:, t0 * ROW:(t0 + gt) * ROW], in_=o_tiles[c][:, lo:lo + gt * ROW])
            elif g == c_last[c]:
                nc.sync.dma_start(out=out_v[:, c_start[c] * ROW:(c_start[c] + CHUNKS[c]) * ROW], in_=o_tiles[c][:])
            if g == c_last[c] and c + LOAD_BUFS < n_chunks:
                load(c + LOAD_BUFS)

        softmax_max(0, HEAD_TILES)
        softmax_shift(0, HEAD_TILES)
        softmax_exp(0, HEAD_TILES)
        softmax_max(HEAD_TILES, TILES)
        softmax_norm(0, HEAD_TILES)
        softmax_shift(HEAD_TILES, TILES)

        w_grouped = const.tile([P, PASSES * P * PACK], BF16, align_bytes=64)
        copy_out(
            transpose_words(w_sb[:].bitcast(F32), 0),
            w_grouped[:].bitcast(F32).rearrange("p (m r u) -> p m r u", m=PASSES, u=2),
        )
        w_codes = const.tile([P, PASSES * P], U32, align_bytes=64)
        w_scales = const.tile([P, PASSES * P], U8, align_bytes=64)
        nc.vector.quantize_mx(out=w_codes[:].bitcast(FP8X4), scales=w_scales[:], in_=w_grouped[:])
        bias = const.tile([P, 1], F32)
        nc.vector.tensor_copy(out=bias[:], in_=b_sb[:])

        for k in range(-3, n_groups):
            if k >= 1:
                store(k - 1)
            if k + 3 < n_groups:
                transposes(k + 3)
            if 0 <= k + 1 < n_groups:
                add_bias(k + 1)
                back_transposes(k + 1)
            if 0 <= k + 2 < n_groups:
                quantise(k + 2)
                mx_passes(k + 2)
            if k == -2:
                softmax_exp(HEAD_TILES, TILES)
            if k == -1:
                softmax_norm(HEAD_TILES, TILES)
            if 0 <= k + 1 < n_groups:
                seed_lower_cells(k + 1)
            if k + 3 < n_groups:
                copies_out(k + 3)
            if 0 <= k + 1 < n_groups:
                seed_top_cells(k + 1)
            if k >= 0:
                blend(k)
        store(n_groups - 1)
